import numpy as np
import ml_dtypes


def mxq(x, axis, fmt="e4m3"):
    dtype, down = {"e4m3": (ml_dtypes.float8_e4m3fn, 7), "e5m2": (ml_dtypes.float8_e5m2, 14)}[fmt]
    v = np.moveaxis(np.asarray(x, np.float32).astype(ml_dtypes.bfloat16).astype(np.float64), axis, -1)
    blocks = v.reshape(v.shape[:-1] + (-1, 32))
    amax = np.abs(blocks).max(-1, keepdims=True)
    byte = np.maximum(np.where(amax > 0, np.frexp(amax)[1] - 1 + 127, 0) - down, 1)
    scale = np.exp2(byte - 127.0)
    codes = (blocks / scale).astype(np.float32).astype(dtype).astype(np.float64)
    return np.moveaxis((codes * scale).reshape(v.shape), -1, axis)


WIDE = False


def mx_kscale(k):
    if not WIDE:
        return np.ones(k)
    levels = np.array([20, -20, 10, -10, 0])
    a = np.random.permutation(np.resize(levels, k // 512 * 4)).reshape(k // 512, 4)
    idx = np.arange(k)
    return np.exp2(a[idx // 512, idx % 128 // 32])


BF16 = ml_dtypes.bfloat16


def bf(x):
    return np.asarray(x, np.float32).astype(BF16)


def f64(x):
    return np.asarray(x).astype(np.float64)


B, T, D, F = 2, 256, 64, 1024
BINS = np.array([-1.5, -1.0, -0.5, 0.0, 0.5, 1.0, 1.5])
NB = BINS.shape[0] + 1
INDEX = 0


def buckets(x):
    y = x[..., INDEX]
    return np.sum(np.where(y[..., None] > BINS, 1.0, 0.0), axis=-1).reshape(B * T)


def setup_inputs():
    u = mx_kscale(F)
    x = np.random.standard_normal((B, T, D))
    W = np.random.standard_normal((NB, D, F)) * 0.5 / np.sqrt(D) / u[None, None, :]
    g = np.random.standard_normal((B, T, F)) * np.exp2(np.random.randint(-12, 1, (B, T, 1))) * 16.0 * u
    y = x[..., INDEX]
    near = np.min(np.abs(y[..., None] - BINS), axis=-1) < 0.01
    x[..., INDEX] = np.where(near, y + 0.03, y)
    return {"x": bf(x), "W": bf(W), "grad_out": bf(g)}


def reference(x, W, grad_out):
    x, W, g = f64(x), f64(W), f64(grad_out)
    memf = buckets(x)
    gq = mxq(g.reshape(B * T, F), 1, "e5m2")
    Wq = mxq(W, 2, "e4m3")
    out = np.zeros((B * T, D))
    for k in range(NB):
        sel = np.where(memf == k, 1.0, 0.0)[:, None]
        out = out + sel * (gq @ Wq[k].T)
    return out.reshape(B, T, D)

@@ -1,0 +1,143 @@
+import concourse.mybir as mybir
+from concourse.masks import make_identity
+
+F32 = mybir.dt.float32
+BF16 = mybir.dt.bfloat16
+U32 = mybir.dt.uint32
+U8 = mybir.dt.uint8
+E4M3_X4 = mybir.dt.float8_e4m3fn_x4
+E5M2_X4 = mybir.dt.float8_e5m2_x4
+ALU = mybir.AluOpType
+
+P = 128
+PACK = 4
+K_PASS = P * PACK
+HALVES = 2
+
+TOKENS = 512
+D = 64
+F = 1024
+EDGES = (-1.5, -1.0, -0.5, 0.0, 0.5, 1.0, 1.5)
+NB = len(EDGES) + 1
+
+PASSES = F // K_PASS
+TOKEN_TILES = TOKENS // P
+W_ROWS = NB * D
+W_CHUNKS = W_ROWS // P
+GROUP = P * PACK
+
+FLOPS = 2 * TOKENS * W_ROWS * F
+BYTES = 2 * (TOKENS + W_ROWS) * F + 2 * TOKENS + 4 * TOKENS * D
+
+
+def transpose_and_quantise(nc, banks, stage, rows, identity, x4, codes, scales):
+    words = rows[:].bitcast(F32)
+    flipped = banks.tile([P, PASSES, HALVES, P], F32)
+    for g in range(PASSES):
+        for u in range(HALVES):
+            first = (g * HALVES + u) * P
+            nc.tensor.transpose(flipped[:, g, u, :], words[:, first : first + P], identity[:])
+    grouped = stage.tile([P, PASSES * GROUP], BF16, align_bytes=64)
+    nc.scalar.copy(
+        out=grouped[:].bitcast(F32).rearrange("q (g r u) -> q g r u", g=PASSES, u=HALVES),
+        in_=flipped[:].rearrange("q g u r -> q g r u"),
+    )
+    for g in range(PASSES):
+        nc.vector.quantize_mx(
+            out=codes[:, g, :].bitcast(x4),
+            scales=scales[:, g, :],
+            in_=grouped[:, g * GROUP : (g + 1) * GROUP],
+        )
+
+
+def tile_dispatchbyvariable_pa_s_kernel(tc, x, W, grad_out, out):
+    nc = tc.nc
+    x_view = x.rearrange("b t d -> (b t) d").rearrange("(p n) d -> p n d", n=TOKEN_TILES)
+    g_view = grad_out.rearrange("b t f -> (b t) f").rearrange("(p n) f -> p n f", n=TOKEN_TILES)
+    out_view = out.rearrange("b t d -> (b t) d").rearrange("(p n) d -> p n d", n=TOKEN_TILES)
+    w_view = W.rearrange("k d f -> (k d) f").rearrange("(c p) f -> p c f", p=P)
+
+    with (
+        tc.tile_pool(name="keep", bufs=1) as keep,
+        tc.tile_pool(name="raw", bufs=W_CHUNKS + TOKEN_TILES) as raw,
+        tc.tile_pool(name="stage", bufs=4) as stage,
+        tc.psum_pool(name="banks", bufs=4) as banks,
+        tc.psum_pool(name="sums", bufs=4) as sums,
+    ):
+        x_sb = keep.tile([P, TOKEN_TILES, D], BF16)
+        nc.sync.dma_start(out=x_sb[:], in_=x_view)
+        w_rows = []
+        for c in range(W_CHUNKS):
+            rows = raw.tile([P, F], BF16)
+            nc.sync.dma_start(out=rows[:], in_=w_view[:, c, :])
+            w_rows.append(rows)
+        g_rows = []
+        for n in range(TOKEN_TILES):
+            rows = raw.tile([P, F], BF16)
+            nc.sync.dma_start(out=rows[:], in_=g_view[:, n, :])
+            g_rows.append(rows)
+
+        identity = keep.tile([P, P], F32)
+        make_identity(nc, identity[:])
+
+        edges = keep.tile([P, len(EDGES)], F32)
+        for j, edge in enumerate(EDGES):
+            nc.vector.memset(edges[:, j : j + 1], edge)
+        above = keep.tile([P, TOKEN_TILES, NB + 1], F32)
+        nc.vector.memset(above[:, :, 0:1], 1.0)
+        nc.vector.memset(above[:, :, NB : NB + 1], 0.0)
+        nc.vector.tensor_tensor(
+            out=above[:, :, 1:NB],
+            in0=x_sb[:, :, 0:1].to_broadcast([P, TOKEN_TILES, len(EDGES)]),
+            in1=edges[:].unsqueeze(1).to_broadcast([P, TOKEN_TILES, len(EDGES)]),
+            op=ALU.is_gt,
+        )
+        chosen = keep.tile([P, TOKEN_TILES, NB], F32)
+        nc.vector.tensor_sub(out=chosen[:], in0=above[:, :, 0:NB], in1=above[:, :, 1 : NB + 1])
+
+        w_codes = keep.tile([P, PASSES, W_ROWS], U32, align_bytes=64)
+        w_scales = keep.tile([P, PASSES, W_ROWS], U8, align_bytes=64)
+        g_codes = keep.tile([P, TOKEN_TILES, PASSES, P], U32, align_bytes=64)
+        g_scales = keep.tile([P, TOKEN_TILES, PASSES, P], U8, align_bytes=64)
+
+        def prepare_w(c):
+            cols = slice(c * P, (c + 1) * P)
+            transpose_and_quantise(
+                nc, banks, stage, w_rows[c], identity, E4M3_X4, w_codes[:, :, cols], w_scales[:, :, cols]
+            )
+
+        def prepare_tokens(n):
+            transpose_and_quantise(
+                nc, banks, stage, g_rows[n], identity, E5M2_X4, g_codes[:, n, :, :], g_scales[:, n, :, :]
+            )
+
+        def multiply_and_pick(n):
+            products = sums.tile([P, W_ROWS], F32)
+            for g in range(PASSES):
+                nc.tensor.matmul_mx(
+                    out=products[:],
+                    lhsT=g_codes[:, n, g, :].bitcast(E5M2_X4),
+                    lhsT_scale=g_scales[:, n, g, :],
+                    rhs=w_codes[:, g, :].bitcast(E4M3_X4),
+                    rhs_scale=w_scales[:, g, :],
+                    start=(g == 0),
+                    stop=(g == PASSES - 1),
+                )
+            picked = stage.tile([P, D, NB], F32)
+            nc.vector.tensor_tensor(
+                out=picked[:],
+                in0=products[:].rearrange("p (k d) -> p d k", k=NB),
+                in1=chosen[:, n, :].unsqueeze(1).to_broadcast([P, D, NB]),
+                op=ALU.mult,
+            )
+            result = stage.tile([P, D], F32)
+            nc.vector.tensor_reduce(out=result[:], in_=picked[:], axis=mybir.AxisListType.X, op=ALU.add)
+            nc.sync.dma_start(out=out_view[:, n, :], in_=result[:])
+
+        for c in range(W_CHUNKS):
+            prepare_w(c)
+        prepare_tokens(0)
+        for n in range(TOKEN_TILES):
+            if n + 1 < TOKEN_TILES:
+                prepare_tokens(n + 1)
+            multiply_and_pick(n)

@@ -24,6 +24,8 @@ PASSES = F // K_PASS
 TOKEN_TILES = TOKENS // P
 W_ROWS = NB * D
 W_CHUNKS = W_ROWS // P
+LEVELS = 3
+WARM_TRANSPOSES = 10
 GROUP = P * PACK
 
 FLOPS = 2 * TOKENS * W_ROWS * F
@@ -80,6 +82,10 @@ def tile_dispatchbyvariable_pa_s_kernel(tc, x, W, grad_out, out):
         identity = keep.tile([P, P], F32)
         make_identity(nc, identity[:])
 
+        warm = banks.tile([P, PASSES, HALVES, P], F32, tag="flipped")
+        for i in range(WARM_TRANSPOSES):
+            nc.tensor.transpose(warm[:, i % PASSES, (i // PASSES) % HALVES, :], identity[:], identity[:])
+
         edges = keep.tile([P, len(EDGES)], F32)
         for j, edge in enumerate(EDGES):
             nc.vector.memset(edges[:, j : j + 1], edge)
@@ -94,6 +100,13 @@ def tile_dispatchbyvariable_pa_s_kernel(tc, x, W, grad_out, out):
         )
         chosen = keep.tile([P, TOKEN_TILES, NB], F32)
         nc.vector.tensor_sub(out=chosen[:], in0=above[:, :, 0:NB], in1=above[:, :, 1 : NB + 1])
+        bits = chosen[:].rearrange("p n (u v w) -> p n u v w", u=2, v=2, w=2)
+        upper = keep.tile([P, LEVELS, TOKEN_TILES], F32)
+        nc.vector.tensor_reduce(out=upper[:, 0, :], in_=bits[:, :, 1, :, :], axis=mybir.AxisListType.XY, op=ALU.add)
+        nc.vector.tensor_reduce(out=upper[:, 1, :], in_=bits[:, :, :, 1, :], axis=mybir.AxisListType.XY, op=ALU.add)
+        nc.vector.tensor_reduce(out=upper[:, 2, :], in_=bits[:, :, :, :, 1], axis=mybir.AxisListType.XY, op=ALU.add)
+        lower = keep.tile([P, LEVELS, TOKEN_TILES], F32)
+        nc.vector.tensor_scalar(out=lower[:], in0=upper[:], scalar1=-1.0, scalar2=1.0, op0=ALU.mult, op1=ALU.add)
 
         w_codes = keep.tile([P, PASSES, W_ROWS], U32, align_bytes=64)
         w_scales = keep.tile([P, PASSES, W_ROWS], U8, align_bytes=64)
@@ -123,15 +136,28 @@ def tile_dispatchbyvariable_pa_s_kernel(tc, x, W, grad_out, out):
                     start=(g == 0),
                     stop=(g == PASSES - 1),
                 )
-            picked = stage.tile([P, D, NB], F32)
-            nc.vector.tensor_tensor(
-                out=picked[:],
-                in0=products[:].rearrange("p (k d) -> p d k", k=NB),
-                in1=chosen[:, n, :].unsqueeze(1).to_broadcast([P, D, NB]),
-                op=ALU.mult,
-            )
-            result = stage.tile([P, D], F32)
-            nc.vector.tensor_reduce(out=result[:], in_=picked[:], axis=mybir.AxisListType.X, op=ALU.add)
+            candidates = products
+            width = W_ROWS
+            for level in range(LEVELS):
+                width = width // 2
+                low = stage.tile([P, width], F32, tag="low%d" % level)
+                nc.scalar.activation(
+                    out=low[:],
+                    in_=candidates[:, 0:width],
+                    func=mybir.ActivationFunctionType.Copy,
+                    scale=lower[:, level, n : n + 1],
+                )
+                kept = stage.tile([P, width], F32, tag="kept%d" % level)
+                nc.vector.scalar_tensor_tensor(
+                    out=kept[:],
+                    in0=candidates[:, width : 2 * width],
+                    scalar=upper[:, level, n : n + 1],
+                    in1=low[:],
+                    op0=ALU.mult,
+                    op1=ALU.add,
+                )
+                candidates = kept
+            result = candidates
             nc.sync.dma_start(out=out_view[:, n, :], in_=result[:])
 
         for c in range(W_CHUNKS):

@@ -25,7 +25,7 @@ TOKEN_TILES = TOKENS // P
 W_ROWS = NB * D
 W_CHUNKS = W_ROWS // P
 LEVELS = 3
-WARM_TRANSPOSES = 10
+WARM_MATMULS = 4
 GROUP = P * PACK
 
 FLOPS = 2 * TOKENS * W_ROWS * F
@@ -64,7 +64,9 @@ def tile_dispatchbyvariable_pa_s_kernel(tc, x, W, grad_out, out):
         tc.tile_pool(name="raw", bufs=W_CHUNKS + TOKEN_TILES) as raw,
         tc.tile_pool(name="stage", bufs=4) as stage,
         tc.psum_pool(name="banks", bufs=4) as banks,
-        tc.psum_pool(name="sums", bufs=4) as sums,
+        tc.psum_pool(name="sums", bufs=3) as sums,
+        tc.psum_pool(name="idle", bufs=1) as idle,
+        tc.manual_schedule(engines={mybir.EngineType.PE}),
     ):
         x_sb = keep.tile([P, TOKEN_TILES, D], BF16)
         nc.sync.dma_start(out=x_sb[:], in_=x_view)
@@ -82,9 +84,13 @@ def tile_dispatchbyvariable_pa_s_kernel(tc, x, W, grad_out, out):
         identity = keep.tile([P, P], F32)
         make_identity(nc, identity[:])
 
-        warm = banks.tile([P, PASSES, HALVES, P], F32, tag="flipped")
-        for i in range(WARM_TRANSPOSES):
-            nc.tensor.transpose(warm[:, i % PASSES, (i // PASSES) % HALVES, :], identity[:], identity[:])
+        unread = idle.tile([P, P], F32)
+
+        def keep_clock_up():
+            nc.tensor.matmul(out=unread[:], lhsT=identity[:], rhs=identity[:], start=True, stop=True)
+
+        for i in range(WARM_MATMULS):
+            keep_clock_up()
 
         edges = keep.tile([P, len(EDGES)], F32)
         for j, edge in enumerate(EDGES):
@@ -162,8 +168,9 @@ def tile_dispatchbyvariable_pa_s_kernel(tc, x, W, grad_out, out):
 
         for c in range(W_CHUNKS):
             prepare_w(c)
-        prepare_tokens(0)
+            keep_clock_up()
         for n in range(TOKEN_TILES):
-            if n + 1 < TOKEN_TILES:
-                prepare_tokens(n + 1)
+            prepare_tokens(n)
+            keep_clock_up()
+        for n in range(TOKEN_TILES):
             multiply_and_pick(n)

@@ -64,10 +64,12 @@ def tile_dispatchbyvariable_pa_s_kernel(tc, x, W, grad_out, out):
         tc.tile_pool(name="raw", bufs=W_CHUNKS + TOKEN_TILES) as raw,
         tc.tile_pool(name="stage", bufs=4) as stage,
         tc.psum_pool(name="banks", bufs=4) as banks,
-        tc.psum_pool(name="sums", bufs=3) as sums,
-        tc.psum_pool(name="idle", bufs=1) as idle,
+        tc.psum_pool(name="sums", bufs=4) as sums,
         tc.manual_schedule(engines={mybir.EngineType.PE}),
     ):
+        zeros = keep.tile([P, P], F32)
+        nc.vector.memset(zeros[:], 0.0)
+
         x_sb = keep.tile([P, TOKEN_TILES, D], BF16)
         nc.sync.dma_start(out=x_sb[:], in_=x_view)
         w_rows = []
@@ -84,10 +86,10 @@ def tile_dispatchbyvariable_pa_s_kernel(tc, x, W, grad_out, out):
         identity = keep.tile([P, P], F32)
         make_identity(nc, identity[:])
 
-        unread = idle.tile([P, P], F32)
+        unread = sums.tile([P, P], F32, tag="products")
 
         def keep_clock_up():
-            nc.tensor.matmul(out=unread[:], lhsT=identity[:], rhs=identity[:], start=True, stop=True)
+            nc.tensor.matmul(out=unread[:], lhsT=zeros[:], rhs=zeros[:], start=True, stop=True)
 
         for i in range(WARM_MATMULS):
             keep_clock_up()
@@ -131,7 +133,7 @@ def tile_dispatchbyvariable_pa_s_kernel(tc, x, W, grad_out, out):
             )
 
         def multiply_and_pick(n):
-            products = sums.tile([P, W_ROWS], F32)
+            products = sums.tile([P, W_ROWS], F32, tag="products")
             for g in range(PASSES):
                 nc.tensor.matmul_mx(
                     out=products[:],
@@ -171,6 +173,7 @@ def tile_dispatchbyvariable_pa_s_kernel(tc, x, W, grad_out, out):
             keep_clock_up()
         for n in range(TOKEN_TILES):
             prepare_tokens(n)
-            keep_clock_up()
+            if n + 1 < TOKEN_TILES:
+                keep_clock_up()
         for n in range(TOKEN_TILES):
             multiply_and_pick(n)

@@ -173,7 +173,7 @@ def tile_dispatchbyvariable_pa_s_kernel(tc, x, W, grad_out, out):
             keep_clock_up()
         for n in range(TOKEN_TILES):
             prepare_tokens(n)
-            if n + 1 < TOKEN_TILES:
+            if n + 2 < TOKEN_TILES:
                 keep_clock_up()
         for n in range(TOKEN_TILES):
             multiply_and_pick(n)

@@ -144,28 +144,30 @@ def tile_dispatchbyvariable_pa_s_kernel(tc, x, W, grad_out, out):
                     start=(g == 0),
                     stop=(g == PASSES - 1),
                 )
-            candidates = products
-            width = W_ROWS
-            for level in range(LEVELS):
-                width = width // 2
-                low = stage.tile([P, width], F32, tag="low%d" % level)
+            half = NB // 2
+            lows = stage.tile([P, half, D], F32)
+            for j in range(half):
                 nc.scalar.activation(
-                    out=low[:],
-                    in_=candidates[:, 0:width],
+                    out=lows[:, j, :],
+                    in_=products[:, j * D : (j + 1) * D],
                     func=mybir.ActivationFunctionType.Copy,
-                    scale=lower[:, level, n : n + 1],
+                    scale=chosen[:, n, j : j + 1],
                 )
-                kept = stage.tile([P, width], F32, tag="kept%d" % level)
+            pairs = stage.tile([P, half, D], F32)
+            for j in range(half):
+                k = half + j
                 nc.vector.scalar_tensor_tensor(
-                    out=kept[:],
-                    in0=candidates[:, width : 2 * width],
-                    scalar=upper[:, level, n : n + 1],
-                    in1=low[:],
+                    out=pairs[:, j, :],
+                    in0=products[:, k * D : (k + 1) * D],
+                    scalar=chosen[:, n, k : k + 1],
+                    in1=lows[:, j, :],
                     op0=ALU.mult,
                     op1=ALU.add,
                 )
-                candidates = kept
-            result = candidates
+            result = stage.tile([P, D], F32)
+            nc.vector.tensor_reduce(
+                out=result[:], in_=pairs[:].rearrange("p j d -> p d j"), axis=mybir.AxisListType.X, op=ALU.add
+            )
             nc.sync.dma_start(out=out_view[:, n, :], in_=result[:])
 
         for c in range(W_CHUNKS):

@@ -65,7 +65,7 @@ def tile_dispatchbyvariable_pa_s_kernel(tc, x, W, grad_out, out):
         tc.tile_pool(name="stage", bufs=4) as stage,
         tc.psum_pool(name="banks", bufs=4) as banks,
         tc.psum_pool(name="sums", bufs=4) as sums,
-        tc.manual_schedule(engines={mybir.EngineType.PE}),
+        tc.manual_schedule(),
     ):
         zeros = keep.tile([P, P], F32)
         nc.vector.memset(zeros[:], 0.0)
@@ -132,7 +132,12 @@ def tile_dispatchbyvariable_pa_s_kernel(tc, x, W, grad_out, out):
                 nc, banks, stage, g_rows[n], identity, E5M2_X4, g_codes[:, n, :, :], g_scales[:, n, :, :]
             )
 
-        def multiply_and_pick(n):
+        products_of = {}
+        lows_of = {}
+        pairs_of = {}
+        half = NB // 2
+
+        def multiply(n):
             products = sums.tile([P, W_ROWS], F32, tag="products")
             for g in range(PASSES):
                 nc.tensor.matmul_mx(
@@ -144,29 +149,37 @@ def tile_dispatchbyvariable_pa_s_kernel(tc, x, W, grad_out, out):
                     start=(g == 0),
                     stop=(g == PASSES - 1),
                 )
-            half = NB // 2
+            products_of[n] = products
+
+        def mask_lower(n):
             lows = stage.tile([P, half, D], F32)
             for j in range(half):
                 nc.scalar.activation(
                     out=lows[:, j, :],
-                    in_=products[:, j * D : (j + 1) * D],
+                    in_=products_of[n][:, j * D : (j + 1) * D],
                     func=mybir.ActivationFunctionType.Copy,
                     scale=chosen[:, n, j : j + 1],
                 )
+            lows_of[n] = lows
+
+        def mask_upper_and_add(n):
             pairs = stage.tile([P, half, D], F32)
             for j in range(half):
                 k = half + j
                 nc.vector.scalar_tensor_tensor(
                     out=pairs[:, j, :],
-                    in0=products[:, k * D : (k + 1) * D],
+                    in0=products_of[n][:, k * D : (k + 1) * D],
                     scalar=chosen[:, n, k : k + 1],
-                    in1=lows[:, j, :],
+                    in1=lows_of[n][:, j, :],
                     op0=ALU.mult,
                     op1=ALU.add,
                 )
+            pairs_of[n] = pairs
+
+        def add_up_and_store(n):
             result = stage.tile([P, D], F32)
             nc.vector.tensor_reduce(
-                out=result[:], in_=pairs[:].rearrange("p j d -> p d j"), axis=mybir.AxisListType.X, op=ALU.add
+                out=result[:], in_=pairs_of[n][:].rearrange("p j d -> p d j"), axis=mybir.AxisListType.X, op=ALU.add
             )
             nc.sync.dma_start(out=out_view[:, n, :], in_=result[:])
 
@@ -178,4 +191,11 @@ def tile_dispatchbyvariable_pa_s_kernel(tc, x, W, grad_out, out):
             if n + 2 < TOKEN_TILES:
                 keep_clock_up()
         for n in range(TOKEN_TILES):
-            multiply_and_pick(n)
+            multiply(n)
+        for step in range(TOKEN_TILES + 2):
+            if step < TOKEN_TILES:
+                mask_lower(step)
+            if 0 <= step - 1 < TOKEN_TILES:
+                mask_upper_and_add(step - 1)
+            if 0 <= step - 2 < TOKEN_TILES:
+                add_up_and_store(step - 2)

@@ -24,7 +24,6 @@ PASSES = F // K_PASS
 TOKEN_TILES = TOKENS // P
 W_ROWS = NB * D
 W_CHUNKS = W_ROWS // P
-LEVELS = 3
 WARM_MATMULS = 4
 GROUP = P * PACK
 
@@ -52,6 +51,19 @@ def transpose_and_quantise(nc, banks, stage, rows, identity, x4, codes, scales):
         )
 
 
+def transpose_and_quantise_pass(nc, banks, stage, half_rows, identity, x4, codes, scales):
+    words = half_rows[:].bitcast(F32)
+    flipped = banks.tile([P, HALVES, P], F32, tag="flipped")
+    for u in range(HALVES):
+        nc.tensor.transpose(flipped[:, u, :], words[:, u * P : (u + 1) * P], identity[:])
+    grouped = stage.tile([P, GROUP], BF16, align_bytes=64, tag="grouped_pass")
+    nc.scalar.copy(
+        out=grouped[:].bitcast(F32).rearrange("q (r u) -> q r u", u=HALVES),
+        in_=flipped[:].rearrange("q u r -> q r u"),
+    )
+    nc.vector.quantize_mx(out=codes.bitcast(x4), scales=scales, in_=grouped[:])
+
+
 def tile_dispatchbyvariable_pa_s_kernel(tc, x, W, grad_out, out):
     nc = tc.nc
     x_view = x.rearrange("b t d -> (b t) d").rearrange("(p n) d -> p n d", n=TOKEN_TILES)
@@ -70,18 +82,23 @@ def tile_dispatchbyvariable_pa_s_kernel(tc, x, W, grad_out, out):
         zeros = keep.tile([P, P], F32)
         nc.vector.memset(zeros[:], 0.0)
 
-        x_sb = keep.tile([P, TOKEN_TILES, D], BF16)
-        nc.sync.dma_start(out=x_sb[:], in_=x_view)
         w_rows = []
         for c in range(W_CHUNKS):
             rows = raw.tile([P, F], BF16)
             nc.sync.dma_start(out=rows[:], in_=w_view[:, c, :])
             w_rows.append(rows)
         g_rows = []
-        for n in range(TOKEN_TILES):
+        for n in range(TOKEN_TILES - 1):
             rows = raw.tile([P, F], BF16)
             nc.sync.dma_start(out=rows[:], in_=g_view[:, n, :])
             g_rows.append(rows)
+        last_halves = []
+        for g in range(PASSES):
+            half_rows = raw.tile([P, K_PASS], BF16)
+            nc.sync.dma_start(out=half_rows[:], in_=g_view[:, TOKEN_TILES - 1, g * K_PASS : (g + 1) * K_PASS])
+            last_halves.append(half_rows)
+        x_sb = keep.tile([P, TOKEN_TILES, D], BF16)
+        nc.sync.dma_start(out=x_sb[:], in_=x_view)
 
         identity = keep.tile([P, P], F32)
         make_identity(nc, identity[:])
@@ -100,21 +117,16 @@ def tile_dispatchbyvariable_pa_s_kernel(tc, x, W, grad_out, out):
         above = keep.tile([P, TOKEN_TILES, NB + 1], F32)
         nc.vector.memset(above[:, :, 0:1], 1.0)
         nc.vector.memset(above[:, :, NB : NB + 1], 0.0)
-        nc.vector.tensor_tensor(
-            out=above[:, :, 1:NB],
-            in0=x_sb[:, :, 0:1].to_broadcast([P, TOKEN_TILES, len(EDGES)]),
-            in1=edges[:].unsqueeze(1).to_broadcast([P, TOKEN_TILES, len(EDGES)]),
-            op=ALU.is_gt,
-        )
         chosen = keep.tile([P, TOKEN_TILES, NB], F32)
-        nc.vector.tensor_sub(out=chosen[:], in0=above[:, :, 0:NB], in1=above[:, :, 1 : NB + 1])
-        bits = chosen[:].rearrange("p n (u v w) -> p n u v w", u=2, v=2, w=2)
-        upper = keep.tile([P, LEVELS, TOKEN_TILES], F32)
-        nc.vector.tensor_reduce(out=upper[:, 0, :], in_=bits[:, :, 1, :, :], axis=mybir.AxisListType.XY, op=ALU.add)
-        nc.vector.tensor_reduce(out=upper[:, 1, :], in_=bits[:, :, :, 1, :], axis=mybir.AxisListType.XY, op=ALU.add)
-        nc.vector.tensor_reduce(out=upper[:, 2, :], in_=bits[:, :, :, :, 1], axis=mybir.AxisListType.XY, op=ALU.add)
-        lower = keep.tile([P, LEVELS, TOKEN_TILES], F32)
-        nc.vector.tensor_scalar(out=lower[:], in0=upper[:], scalar1=-1.0, scalar2=1.0, op0=ALU.mult, op1=ALU.add)
+
+        def find_buckets():
+            nc.vector.tensor_tensor(
+                out=above[:, :, 1:NB],
+                in0=x_sb[:, :, 0:1].to_broadcast([P, TOKEN_TILES, len(EDGES)]),
+                in1=edges[:].unsqueeze(1).to_broadcast([P, TOKEN_TILES, len(EDGES)]),
+                op=ALU.is_gt,
+            )
+            nc.vector.tensor_sub(out=chosen[:], in0=above[:, :, 0:NB], in1=above[:, :, 1 : NB + 1])
 
         w_codes = keep.tile([P, PASSES, W_ROWS], U32, align_bytes=64)
         w_scales = keep.tile([P, PASSES, W_ROWS], U8, align_bytes=64)
@@ -128,6 +140,12 @@ def tile_dispatchbyvariable_pa_s_kernel(tc, x, W, grad_out, out):
             )
 
         def prepare_tokens(n):
+            if n == TOKEN_TILES - 1:
+                for g in range(PASSES):
+                    transpose_and_quantise_pass(
+                        nc, banks, stage, last_halves[g], identity, E5M2_X4, g_codes[:, n, g, :], g_scales[:, n, g, :]
+                    )
+                return
             transpose_and_quantise(
                 nc, banks, stage, g_rows[n], identity, E5M2_X4, g_codes[:, n, :, :], g_scales[:, n, :, :]
             )
@@ -190,6 +208,8 @@ def tile_dispatchbyvariable_pa_s_kernel(tc, x, W, grad_out, out):
             prepare_tokens(n)
             if n + 2 < TOKEN_TILES:
                 keep_clock_up()
+            if n == 1:
+                find_buckets()
         for n in range(TOKEN_TILES):
             multiply(n)
         for step in range(TOKEN_TILES + 2):

import concourse.mybir as mybir
from concourse.masks import make_identity

F32 = mybir.dt.float32
BF16 = mybir.dt.bfloat16
U32 = mybir.dt.uint32
U8 = mybir.dt.uint8
E4M3_X4 = mybir.dt.float8_e4m3fn_x4
E5M2_X4 = mybir.dt.float8_e5m2_x4
ALU = mybir.AluOpType

P = 128
PACK = 4
K_PASS = P * PACK
HALVES = 2

TOKENS = 512
D = 64
F = 1024
EDGES = (-1.5, -1.0, -0.5, 0.0, 0.5, 1.0, 1.5)
NB = len(EDGES) + 1

PASSES = F // K_PASS
TOKEN_TILES = TOKENS // P
W_ROWS = NB * D
W_CHUNKS = W_ROWS // P
WARM_MATMULS = 4
GROUP = P * PACK

FLOPS = 2 * TOKENS * W_ROWS * F
BYTES = 2 * (TOKENS + W_ROWS) * F + 2 * TOKENS + 4 * TOKENS * D


def transpose_and_quantise(nc, banks, stage, rows, identity, x4, codes, scales):
    words = rows[:].bitcast(F32)
    flipped = banks.tile([P, PASSES, HALVES, P], F32)
    for g in range(PASSES):
        for u in range(HALVES):
            first = (g * HALVES + u) * P
            nc.tensor.transpose(flipped[:, g, u, :], words[:, first : first + P], identity[:])
    grouped = stage.tile([P, PASSES * GROUP], BF16, align_bytes=64)
    nc.scalar.copy(
        out=grouped[:].bitcast(F32).rearrange("q (g r u) -> q g r u", g=PASSES, u=HALVES),
        in_=flipped[:].rearrange("q g u r -> q g r u"),
    )
    for g in range(PASSES):
        nc.vector.quantize_mx(
            out=codes[:, g, :].bitcast(x4),
            scales=scales[:, g, :],
            in_=grouped[:, g * GROUP : (g + 1) * GROUP],
        )


def transpose_and_quantise_pass(nc, banks, stage, half_rows, identity, x4, codes, scales):
    words = half_rows[:].bitcast(F32)
    flipped = banks.tile([P, HALVES, P], F32, tag="flipped")
    for u in range(HALVES):
        nc.tensor.transpose(flipped[:, u, :], words[:, u * P : (u + 1) * P], identity[:])
    grouped = stage.tile([P, GROUP], BF16, align_bytes=64, tag="grouped_pass")
    nc.scalar.copy(
        out=grouped[:].bitcast(F32).rearrange("q (r u) -> q r u", u=HALVES),
        in_=flipped[:].rearrange("q u r -> q r u"),
    )
    nc.vector.quantize_mx(out=codes.bitcast(x4), scales=scales, in_=grouped[:])


def tile_dispatchbyvariable_pa_s_kernel(tc, x, W, grad_out, out):
    nc = tc.nc
    x_view = x.rearrange("b t d -> (b t) d").rearrange("(p n) d -> p n d", n=TOKEN_TILES)
    g_view = grad_out.rearrange("b t f -> (b t) f").rearrange("(p n) f -> p n f", n=TOKEN_TILES)
    out_view = out.rearrange("b t d -> (b t) d").rearrange("(p n) d -> p n d", n=TOKEN_TILES)
    w_view = W.rearrange("k d f -> (k d) f").rearrange("(c p) f -> p c f", p=P)

    with (
        tc.tile_pool(name="keep", bufs=1) as keep,
        tc.tile_pool(name="raw", bufs=W_CHUNKS + TOKEN_TILES) as raw,
        tc.tile_pool(name="stage", bufs=4) as stage,
        tc.psum_pool(name="banks", bufs=4) as banks,
        tc.psum_pool(name="sums", bufs=4) as sums,
        tc.manual_schedule(),
    ):
        zeros = keep.tile([P, P], F32)
        nc.vector.memset(zeros[:], 0.0)

        w_rows = []
        for c in range(W_CHUNKS):
            rows = raw.tile([P, F], BF16)
            nc.sync.dma_start(out=rows[:], in_=w_view[:, c, :])
            w_rows.append(rows)
        g_rows = []
        for n in range(TOKEN_TILES - 1):
            rows = raw.tile([P, F], BF16)
            nc.sync.dma_start(out=rows[:], in_=g_view[:, n, :])
            g_rows.append(rows)
        last_halves = []
        for g in range(PASSES):
            half_rows = raw.tile([P, K_PASS], BF16)
            nc.sync.dma_start(out=half_rows[:], in_=g_view[:, TOKEN_TILES - 1, g * K_PASS : (g + 1) * K_PASS])
            last_halves.append(half_rows)
        x_sb = keep.tile([P, TOKEN_TILES, D], BF16)
        nc.sync.dma_start(out=x_sb[:], in_=x_view)

        identity = keep.tile([P, P], F32)
        make_identity(nc, identity[:])

        unread = sums.tile([P, P], F32, tag="products")

        def keep_clock_up():
            nc.tensor.matmul(out=unread[:], lhsT=zeros[:], rhs=zeros[:], start=True, stop=True)

        for i in range(WARM_MATMULS):
            keep_clock_up()

        edges = keep.tile([P, len(EDGES)], F32)
        for j, edge in enumerate(EDGES):
            nc.vector.memset(edges[:, j : j + 1], edge)
        above = keep.tile([P, TOKEN_TILES, NB + 1], F32)
        nc.vector.memset(above[:, :, 0:1], 1.0)
        nc.vector.memset(above[:, :, NB : NB + 1], 0.0)
        chosen = keep.tile([P, TOKEN_TILES, NB], F32)

        def find_buckets():
            nc.vector.tensor_tensor(
                out=above[:, :, 1:NB],
                in0=x_sb[:, :, 0:1].to_broadcast([P, TOKEN_TILES, len(EDGES)]),
                in1=edges[:].unsqueeze(1).to_broadcast([P, TOKEN_TILES, len(EDGES)]),
                op=ALU.is_gt,
            )
            nc.vector.tensor_sub(out=chosen[:], in0=above[:, :, 0:NB], in1=above[:, :, 1 : NB + 1])

        w_codes = keep.tile([P, PASSES, W_ROWS], U32, align_bytes=64)
        w_scales = keep.tile([P, PASSES, W_ROWS], U8, align_bytes=64)
        g_codes = keep.tile([P, TOKEN_TILES, PASSES, P], U32, align_bytes=64)
        g_scales = keep.tile([P, TOKEN_TILES, PASSES, P], U8, align_bytes=64)

        def prepare_w(c):
            cols = slice(c * P, (c + 1) * P)
            transpose_and_quantise(
                nc, banks, stage, w_rows[c], identity, E4M3_X4, w_codes[:, :, cols], w_scales[:, :, cols]
            )

        def prepare_tokens(n):
            if n == TOKEN_TILES - 1:
                for g in range(PASSES):
                    transpose_and_quantise_pass(
                        nc, banks, stage, last_halves[g], identity, E5M2_X4, g_codes[:, n, g, :], g_scales[:, n, g, :]
                    )
                return
            transpose_and_quantise(
                nc, banks, stage, g_rows[n], identity, E5M2_X4, g_codes[:, n, :, :], g_scales[:, n, :, :]
            )

        products_of = {}
        lows_of = {}
        pairs_of = {}
        half = NB // 2

        def multiply(n):
            products = sums.tile([P, W_ROWS], F32, tag="products")
            for g in range(PASSES):
                nc.tensor.matmul_mx(
                    out=products[:],
                    lhsT=g_codes[:, n, g, :].bitcast(E5M2_X4),
                    lhsT_scale=g_scales[:, n, g, :],
                    rhs=w_codes[:, g, :].bitcast(E4M3_X4),
                    rhs_scale=w_scales[:, g, :],
                    start=(g == 0),
                    stop=(g == PASSES - 1),
                )
            products_of[n] = products

        def mask_lower(n):
            lows = stage.tile([P, half, D], F32)
            for j in range(half):
                nc.scalar.activation(
                    out=lows[:, j, :],
                    in_=products_of[n][:, j * D : (j + 1) * D],
                    func=mybir.ActivationFunctionType.Copy,
                    scale=chosen[:, n, j : j + 1],
                )
            lows_of[n] = lows

        def mask_upper_and_add(n):
            pairs = stage.tile([P, half, D], F32)
            for j in range(half):
                k = half + j
                nc.vector.scalar_tensor_tensor(
                    out=pairs[:, j, :],
                    in0=products_of[n][:, k * D : (k + 1) * D],
                    scalar=chosen[:, n, k : k + 1],
                    in1=lows_of[n][:, j, :],
                    op0=ALU.mult,
                    op1=ALU.add,
                )
            pairs_of[n] = pairs

        def add_up_and_store(n):
            result = stage.tile([P, D], F32)
            nc.vector.tensor_reduce(
                out=result[:], in_=pairs_of[n][:].rearrange("p j d -> p d j"), axis=mybir.AxisListType.X, op=ALU.add
            )
            nc.sync.dma_start(out=out_view[:, n, :], in_=result[:])

        for c in range(W_CHUNKS):
            prepare_w(c)
            keep_clock_up()
        for n in range(TOKEN_TILES):
            prepare_tokens(n)
            if n + 2 < TOKEN_TILES:
                keep_clock_up()
            if n == 1:
                find_buckets()
        for n in range(TOKEN_TILES):
            multiply(n)
        for step in range(TOKEN_TILES + 2):
            if step < TOKEN_TILES:
                mask_lower(step)
            if 0 <= step - 1 < TOKEN_TILES:
                mask_upper_and_add(step - 1)
            if 0 <= step - 2 < TOKEN_TILES:
                add_up_and_store(step - 2)
